import numpy as np
import ml_dtypes


def mxq(x, axis, fmt="e4m3"):
    dtype, down = {"e4m3": (ml_dtypes.float8_e4m3fn, 7), "e5m2": (ml_dtypes.float8_e5m2, 14)}[fmt]
    v = np.moveaxis(np.asarray(x, np.float32).astype(ml_dtypes.bfloat16).astype(np.float64), axis, -1)
    blocks = v.reshape(v.shape[:-1] + (-1, 32))
    amax = np.abs(blocks).max(-1, keepdims=True)
    byte = np.maximum(np.where(amax > 0, np.frexp(amax)[1] - 1 + 127, 0) - down, 1)
    scale = np.exp2(byte - 127.0)
    codes = (blocks / scale).astype(np.float32).astype(dtype).astype(np.float64)
    return np.moveaxis((codes * scale).reshape(v.shape), -1, axis)


WIDE = False


def mx_kscale(k):
    if not WIDE:
        return np.ones(k)
    levels = np.array([10, -10, 5, -5, 0])
    if k % 512:
        return np.exp2(np.random.permutation(np.resize(levels, k // 32))).repeat(32)
    a = np.empty((k // 512, 16))
    for p in range(k // 512):
        a[p, :8] = np.random.permutation(np.resize(levels, 8))
        for g in range(8):
            far = levels[np.abs(levels - a[p, g]) >= 10]
            a[p, g + 8] = far[np.random.randint(len(far))]
    return np.exp2(a.ravel()).repeat(32)


BF16 = ml_dtypes.bfloat16


def bf(x):
    return np.asarray(x, np.float32).astype(BF16)


def f64(x):
    return np.asarray(x).astype(np.float64)


E2M1 = np.array([0.0, 0.5, 1.0, 1.5, 2.0, 3.0, 4.0, 6.0, -0.0, -0.5, -1.0, -1.5, -2.0, -3.0, -4.0, -6.0])


def pack_weight(w, fmt):
    k, n = w.shape
    w = f64(bf(w)).reshape(k // 32, 32, n)
    amax = np.abs(w).max(1)
    if fmt == "e4m3":
        byte = np.frexp(amax)[1] - 1 + 127 - 7
    else:
        mant, ex = np.frexp(amax / 6.0)
        byte = np.where(mant > 0.5, ex, ex - 1) + 127
    byte = np.clip(np.where(amax > 0, byte, 1), 1, 254)
    scaled = (w * np.exp2(127.0 - byte)[:, None, :]).reshape(k, n).astype(np.float32)
    by_word = np.ascontiguousarray(scaled.reshape(k // 512, 128, 4, n).transpose(0, 1, 3, 2))
    if fmt == "e4m3":
        words = by_word.astype(ml_dtypes.float8_e4m3fn).view(np.uint8)
    else:
        c = by_word.astype(ml_dtypes.float4_e2m1fn).view(np.uint8) & 0xF
        words = c[..., 0::2] | (c[..., 1::2] << 4)
    return np.ascontiguousarray(words), np.ascontiguousarray(byte.astype(np.uint8).reshape(k // 512, 16, n))


def unpack_weight(words, scales, fmt):
    g, p, n, _ = words.shape
    if fmt == "e4m3":
        vals = np.ascontiguousarray(words).view(ml_dtypes.float8_e4m3fn).astype(np.float64)
    else:
        nib = np.empty((g, p, n, 4), np.uint8)
        nib[..., 0::2] = words & 0xF
        nib[..., 1::2] = words >> 4
        vals = E2M1[nib]
    vals = vals * np.repeat(np.exp2(scales.astype(np.float64) - 127.0), 8, axis=1)[..., None]
    return vals.transpose(0, 1, 3, 2).reshape(g * 512, n)


B, S, D, H, DH, DL, DR = 2, 2048, 1024, 2, 128, 512, 64
ROPE_BASE = 10000.0


def rope_cos_sin():
    inv_freq = 1.0 / ROPE_BASE ** (np.arange(0, DR, 2) / DR)
    freqs = np.arange(S)[:, None] * inv_freq[None, :]
    emb = np.concatenate([freqs, freqs], axis=-1)
    return np.cos(emb)[None, :, None, :], np.sin(emb)[None, :, None, :]


def rotate_half(u):
    u1, u2 = np.split(u, 2, axis=-1)
    return np.concatenate([-u2, u1], axis=-1)


def draw0():
    s, t = mx_kscale(D), mx_kscale(DL)
    x = bf(np.random.standard_normal((B, S, D)) * s)
    down_words, down_scales = pack_weight(np.random.standard_normal((D, DL)) / np.sqrt(D) / s[:, None] * t, "e4m3")
    up_words, up_scales = pack_weight(np.random.standard_normal((DL, H * (DH + DR + DH))) / np.sqrt(DL) / t[:, None], "e4m3")
    return {"x": x,
            "W_kv_down_words": down_words, "W_kv_down_scales": down_scales,
            "W_kv_up_words": up_words, "W_kv_up_scales": up_scales}


def core(x, W_kv_down_words, W_kv_down_scales, W_kv_up_words, W_kv_up_scales):
    kv_latent = mxq(f64(x), 2, "e4m3") @ unpack_weight(W_kv_down_words, W_kv_down_scales, "e4m3")
    kv_full = (mxq(kv_latent, 2, "e4m3") @ unpack_weight(W_kv_up_words, W_kv_up_scales, "e4m3")).reshape(B, S, H, DH + DR + DH)
    k_content = kv_full[..., :DH]
    k_rope = kv_full[..., DH:DH + DR]
    v = kv_full[..., DH + DR:]
    cos, sin = rope_cos_sin()
    k_rope = k_rope * cos + rotate_half(k_rope) * sin
    k = np.concatenate([k_content, k_rope], axis=-1)
    return k, v


def e4m3fn_bytes(y):
    return np.clip(np.asarray(y, np.float64), -448.0, 448.0).astype(np.float32).astype(ml_dtypes.float8_e4m3fn).view(np.uint8)


def e4m3fn_values(b):
    return np.asarray(b, np.uint8).view(ml_dtypes.float8_e4m3fn).astype(np.float64)


def setup_inputs():
    d = draw0()
    x0 = np.asarray(d['x']).astype(np.float64)
    s = (np.max(np.abs(x0), axis=(0, 1), keepdims=True) / 448.0).astype(np.float32)
    out = {}
    for k, v in d.items():
        if k == 'x':
            out['x_bytes'] = e4m3fn_bytes(x0 / s.astype(np.float64))
            out['x_scale'] = s
        else:
            out[k] = v
    return out


def reference(x_bytes, x_scale, W_kv_down_words, W_kv_down_scales, W_kv_up_words, W_kv_up_scales):
    return core(e4m3fn_values(x_bytes) * x_scale.astype(np.float64), W_kv_down_words, W_kv_down_scales, W_kv_up_words, W_kv_up_scales)

@@ -1,0 +1,248 @@
+import math
+from contextlib import ExitStack
+
+import concourse.mybir as mybir
+from concourse.masks import make_identity
+
+F32 = mybir.dt.float32
+BF16 = mybir.dt.bfloat16
+I32 = mybir.dt.int32
+U8 = mybir.dt.uint8
+FP8 = mybir.dt.float8_e4m3fn
+FP8X4 = mybir.dt.float8_e4m3fn_x4
+ADD = mybir.AluOpType.add
+SUB = mybir.AluOpType.subtract
+MULT = mybir.AluOpType.mult
+SIN = mybir.ActivationFunctionType.Sin
+
+P = 128
+B, S, D, H, DH, DL, DR = 2, 2048, 1024, 2, 128, 512, 64
+G1 = D // 512
+RUN = S // P
+UT = 2
+TOK = UT * P
+UNITS = B * RUN // UT
+NPOS = RUN // UT
+SLOT = DH + DR
+
+FLOPS = 2 * B * S * (D * DL + DL * H * (2 * DH + DR))
+
+
+def tile_multilatentattention_pa_t_w8_kernel(tc, x_bytes, x_scale, wd_w, wd_s, wu_w, wu_s, out_k, out_v):
+    nc = tc.nc
+    with ExitStack() as ctx:
+        const = ctx.enter_context(tc.tile_pool(name="const", bufs=1))
+        xin = ctx.enter_context(tc.tile_pool(name="xin", bufs=UNITS))
+        work = ctx.enter_context(tc.tile_pool(name="work", bufs=4))
+        stage = ctx.enter_context(tc.tile_pool(name="stage", bufs=4))
+        ps_x = ctx.enter_context(tc.psum_pool(name="ps_x", bufs=3))
+        ps_l = ctx.enter_context(tc.psum_pool(name="ps_l", bufs=2))
+        ps_m = ctx.enter_context(tc.psum_pool(name="ps_m", bufs=2))
+        ps_r = ctx.enter_context(tc.psum_pool(name="ps_r", bufs=1))
+        ctx.enter_context(tc.manual_schedule())
+
+        ident = const.tile([P, P], F32)
+        pos = const.tile([P, RUN], I32)
+        turns = const.tile([P, 2, RUN, DR // 2], F32)
+        whole = const.tile([P, 2, RUN, DR // 2], I32)
+        frac = const.tile([P, 2, RUN, DR // 2], F32)
+        cos_t = const.tile([P, RUN, 2, DR // 2], F32)
+        sin_t = const.tile([P, RUN, 2, DR // 2], F32)
+        dummy = const.tile([P, 1], F32)
+        xsc = const.tile([P, G1, 4], F32)
+        wd_raw = const.tile([P, G1, DL], I32, align_bytes=64)
+        wd = const.tile([P, G1, DL], I32, align_bytes=64)
+        sraw = const.tile([P, DL + 640], U8, align_bytes=64)
+        wds = const.tile([P, DL], U8, align_bytes=64)
+        wu = const.tile([P, 640], I32, align_bytes=64)
+        wus = const.tile([P, 640], U8, align_bytes=64)
+
+        xb, xw, xt, xs, xq, xqs, lt, lat, lq, lqs, mb, rb, st, ra, rs = [{} for _ in range(15)]
+
+        def load_x(u):
+            xb[u] = xin.tile([P, UT, D], U8, name="xb")
+            b, j = divmod(u, NPOS)
+            nc.sync.dma_start(out=xb[u][:], in_=x_bytes[b].rearrange("(r i) k -> r i k", i=RUN)[:, UT * j:UT * (j + 1), :])
+
+        b0 = x_bytes[0].rearrange("(r i) k -> r i k", i=RUN)
+        xb[0] = xin.tile([P, UT, D], U8, name="xb")
+        for i in range(UT):
+            nc.sync.dma_start(out=xb[0][:, i, :], in_=b0[:, i, :])
+        nc.sync.dma_start(out=xsc[:], in_=x_scale.rearrange("a b (g p t) -> p (a b g) t", p=P, t=4))
+        for g in range(G1):
+            nc.sync.dma_start(out=wd_raw[:, g, :], in_=wd_w[g].rearrange("p n t -> p (n t)").bitcast(I32))
+        nc.vector.memset(sraw[:].bitcast(I32), 0)
+        for q in range(4):
+            nc.sync.dma_start(out=sraw[32 * q:32 * q + 8, 0:DL].bitcast(I32), in_=wd_s.bitcast(I32)[:, 4 * q:4 * q + 4, :])
+        for q in range(4):
+            nc.sync.dma_start(out=sraw[32 * q:32 * q + 4, DL:].bitcast(I32), in_=wu_s.bitcast(I32)[0, 4 * q:4 * q + 4, :])
+        load_x(1)
+        wu_v = wu_w[0].rearrange("p n t -> p (n t)").bitcast(I32).rearrange("p (h f) -> p h f", h=H)
+        for c0, c1, f0 in ((0, 256, 0), (256, 512, DH + DR), (512, 640, DH)):
+            w = (c1 - c0) // 2
+            nc.sync.dma_start(out=wu[:, c0:c1].rearrange("p (h d) -> p h d", h=H), in_=wu_v[:, :, f0:f0 + w])
+        for u in range(2, UNITS):
+            load_x(u)
+
+        make_identity(nc, ident[:])
+        nc.gpsimd.iota(pos[:], pattern=[[1, RUN]], base=0, channel_multiplier=RUN)
+        nc.vector.memset(dummy[:], 0.0)
+        nc.scalar.activation(dummy[:], dummy[:], SIN)
+        nc.vector.tensor_scalar(out=turns[:, 0, :, 0], in0=pos[:], scalar1=1.0 / (2.0 * math.pi), scalar2=None, op0=MULT)
+        n = 1
+        while n < DR // 2:
+            nc.gpsimd.tensor_scalar(out=turns[:, 0, :, n:2 * n], in0=turns[:, 0, :, 0:n], scalar1=10000.0 ** (-n / 32.0), scalar2=0.0, op0=MULT, op1=ADD)
+            n *= 2
+        nc.gpsimd.tensor_scalar(out=turns[:, 1], in0=turns[:, 0], scalar1=1.0, scalar2=0.25, op0=MULT, op1=ADD)
+
+        def tables_v():
+            nc.vector.tensor_copy(out=whole[:], in_=turns[:])
+            nc.vector.tensor_tensor(out=frac[:], in0=turns[:], in1=whole[:], op=SUB)
+
+        def tables_s():
+            for half in range(2):
+                nc.scalar.activation(cos_t[:, :, half, :], frac[:, 1], SIN, scale=2.0 * math.pi)
+                nc.scalar.activation(sin_t[:, :, half, :], frac[:, 0], SIN, scale=(2.0 * half - 1.0) * 2.0 * math.pi)
+
+        def permute_wd():
+            for g in range(G1):
+                nc.vector.tensor_copy(out=wd[:, g, :].rearrange("p (t m) -> p t m", t=4), in_=wd_raw[:, g, :].rearrange("p (m t) -> p t m", t=4))
+
+        def permute_scales():
+            nc.vector.tensor_copy(out=wds[:].rearrange("p (t m) -> p t m", t=4), in_=sraw[:, 0:DL].rearrange("p (m t) -> p t m", t=4))
+
+        def permute_wus():
+            sv = sraw[:, DL:].rearrange("p (h f) -> p h f", h=H)
+            for c0, c1, f0 in ((0, 256, 0), (256, 512, DH + DR), (512, 640, DH)):
+                w = (c1 - c0) // 2
+                nc.vector.tensor_copy(out=wus[:, c0:c1].rearrange("p (h d) -> p h d", h=H), in_=sv[:, :, f0:f0 + w])
+
+        def cast(u):
+            xw[u] = work.tile([P, UT, D], BF16, name="xw")
+            for i in range(UT):
+                src = xb[u][:, i, :].bitcast(FP8)
+                if u == 0 and i == 0:
+                    nc.vector.tensor_copy(out=xw[u][:, i, :], in_=src)
+                else:
+                    nc.scalar.copy(out=xw[u][:, i, :], in_=src)
+
+        def transpose(u):
+            for g in range(G1):
+                xt[u, g] = ps_x.tile([P, 2, TOK], F32, name="xt")
+            order = [(g, i) for g in range(G1) for i in range(UT)] if u else [(g, i) for i in range(UT) for g in range(G1)]
+            for g, i in order:
+                    words = xw[u][:, i, :].bitcast(F32)
+                    for w in range(2):
+                        nc.tensor.transpose(xt[u, g][:, w, i * P:(i + 1) * P], words[:, 256 * g + w:256 * (g + 1):2], ident[:])
+
+        def scale(u, g):
+            if g == 0:
+                xs[u] = work.tile([P, G1, TOK, 4], BF16, name="xs", align_bytes=64)
+            nc.vector.tensor_tensor(
+                out=xs[u][:, g].rearrange("p n (w e) -> p n w e", e=2),
+                in0=xt[u, g][:].bitcast(BF16).rearrange("p w (n e) -> p n w e", e=2),
+                in1=xsc[:, g, :].rearrange("p (w e) -> p w e", e=2).unsqueeze(1).to_broadcast([P, TOK, 2, 2]),
+                op=MULT)
+
+        def quantize_x(u, g):
+            if g == 0:
+                xq[u] = work.tile([P, G1, TOK], I32, name="xq", align_bytes=64)
+                xqs[u] = work.tile([P, G1, TOK], U8, name="xqs", align_bytes=64)
+            nc.vector.quantize_mx(out=xq[u][:, g, :].bitcast(FP8X4), scales=xqs[u][:, g, :], in_=xs[u][:, g].rearrange("p n t -> p (n t)"))
+
+        def project_down(u):
+            for i in range(UT):
+                lt[u, i] = ps_l.tile([P, 4, P], F32, name="lt")
+                c = slice(i * P, (i + 1) * P)
+                for t in range(4):
+                    m = slice(t * P, (t + 1) * P)
+                    for g in range(G1):
+                        nc.tensor.matmul_mx(out=lt[u, i][:, t, :], lhsT=wd[:, g, m].bitcast(FP8X4), lhsT_scale=wds[4 * g:P, m],
+                                            rhs=xq[u][:, g, c].bitcast(FP8X4), rhs_scale=xqs[u][:, g, c],
+                                            start=(g == 0), stop=(g == G1 - 1))
+
+        def evac_latent(u):
+            lat[u] = work.tile([P, UT, P, 4], BF16, name="lat", align_bytes=64)
+            for i in range(UT):
+                copy = nc.vector.tensor_copy if u == UNITS - 1 and i == 1 else nc.scalar.copy
+                copy(out=lat[u][:, i], in_=lt[u, i][:].rearrange("p t n -> p n t"))
+
+        def quantize_latent(u):
+            lq[u] = work.tile([P, TOK], I32, name="lq", align_bytes=64)
+            lqs[u] = work.tile([P, TOK], U8, name="lqs", align_bytes=64)
+            nc.vector.quantize_mx(out=lq[u][:].bitcast(FP8X4), scales=lqs[u][:], in_=lat[u][:].rearrange("p i n t -> p (i n t)"))
+
+        def project_up(u):
+            rb[u] = ps_r.tile([P, UT, H * DR], F32, name="rb")
+            for i in range(UT):
+                mb[u, i] = ps_m.tile([P, 512], F32, name="mb")
+                c = slice(i * P, (i + 1) * P)
+                for out, cols in ((rb[u][:, i, :], slice(512, 640)), (mb[u, i][:], slice(0, 512))):
+                    nc.tensor.matmul_mx(out=out, lhsT=lq[u][:, c].bitcast(FP8X4), lhsT_scale=lqs[u][:, c],
+                                        rhs=wu[:, cols].bitcast(FP8X4), rhs_scale=wus[:, cols], start=True, stop=True)
+
+        def evac_main(u):
+            st[u] = stage.tile([P, UT, 4, SLOT], F32, name="st")
+            b, j = divmod(u, NPOS)
+            for i in range(UT):
+                copy = nc.vector.tensor_copy if u == UNITS - 1 and i == 1 else nc.scalar.copy
+                copy(out=st[u][:, i, :, 0:DH], in_=mb[u, i][:].rearrange("p (s d) -> p s d", s=4))
+                nc.sync.dma_start(out=out_v[b].rearrange("(r i) h d -> r i h d", i=RUN)[:, UT * j + i], in_=st[u][:, i, 2:4, 0:DH])
+
+        def rope_mult(u, part):
+            j = u % NPOS
+            v = rb[u][:].rearrange("p i (h a d) -> p i h a d", h=H, a=2)
+            shape = [P, UT, H, 2, DR // 2]
+            if part == 0:
+                ra[u] = work.tile(shape, F32, name="ra")
+                tc_ = cos_t[:, UT * j:UT * (j + 1)].unsqueeze(2).to_broadcast(shape)
+                nc.vector.tensor_tensor(out=ra[u][:], in0=v, in1=tc_, op=MULT)
+            else:
+                rs[u] = work.tile(shape, F32, name="rs")
+                ts_ = sin_t[:, UT * j:UT * (j + 1)].unsqueeze(2).to_broadcast(shape)
+                nc.vector.tensor_tensor(out=rs[u][:], in0=v[:, :, :, ::-1, :], in1=ts_, op=MULT)
+
+        def rope_add(u):
+            b, j = divmod(u, NPOS)
+            nc.gpsimd.tensor_tensor(out=st[u][:, :, 0:2, DH:SLOT], in0=ra[u][:].rearrange("p i h a d -> p i h (a d)"),
+                                    in1=rs[u][:].rearrange("p i h a d -> p i h (a d)"), op=ADD)
+            nc.sync.dma_start(out=out_k[b].rearrange("(r i) h d -> r i (h d)", i=RUN)[:, UT * j:UT * (j + 1), :],
+                              in_=st[u][:, :, 0:2, :].rearrange("p i s d -> p i (s d)"))
+
+        def ok(u):
+            return 0 <= u < UNITS
+
+        cast(0)
+        cast(1)
+        permute_wd()
+        tables_v()
+        transpose(0)
+        tables_s()
+        for s in range(UNITS + 2):
+            if ok(s + 2):
+                cast(s + 2)
+            if ok(s):
+                scale(s, 0)
+                scale(s, 1)
+                if s == 0:
+                    permute_scales()
+                quantize_x(s, 0)
+            if ok(s - 2):
+                rope_mult(s - 2, 0)
+            if ok(s):
+                quantize_x(s, 1)
+            if ok(s - 2):
+                rope_mult(s - 2, 1)
+                rope_add(s - 2)
+            if s == 0:
+                permute_wus()
+            if ok(s - 1):
+                quantize_latent(s - 1)
+            if ok(s + 1):
+                transpose(s + 1)
+            if ok(s):
+                project_down(s)
+                evac_latent(s)
+            if ok(s - 1):
+                project_up(s - 1)
+                evac_main(s - 1)

@@ -24,6 +24,7 @@ TOK = UT * P
 UNITS = B * RUN // UT
 NPOS = RUN // UT
 SLOT = DH + DR
+GPSIMD_CASTS = (3, 4, 6, 8, 9, 11, 13, 15)
 
 FLOPS = 2 * B * S * (D * DL + DL * H * (2 * DH + DR))
 
@@ -34,6 +35,7 @@ def tile_multilatentattention_pa_t_w8_kernel(tc, x_bytes, x_scale, wd_w, wd_s, w
         const = ctx.enter_context(tc.tile_pool(name="const", bufs=1))
         xin = ctx.enter_context(tc.tile_pool(name="xin", bufs=UNITS))
         work = ctx.enter_context(tc.tile_pool(name="work", bufs=4))
+        wide = ctx.enter_context(tc.tile_pool(name="wide", bufs=5))
         stage = ctx.enter_context(tc.tile_pool(name="stage", bufs=4))
         ps_x = ctx.enter_context(tc.psum_pool(name="ps_x", bufs=3))
         ps_l = ctx.enter_context(tc.psum_pool(name="ps_l", bufs=2))
@@ -43,11 +45,13 @@ def tile_multilatentattention_pa_t_w8_kernel(tc, x_bytes, x_scale, wd_w, wd_s, w
 
         ident = const.tile([P, P], F32)
         pos = const.tile([P, RUN], I32)
-        turns = const.tile([P, 2, RUN, DR // 2], F32)
-        whole = const.tile([P, 2, RUN, DR // 2], I32)
-        frac = const.tile([P, 2, RUN, DR // 2], F32)
-        cos_t = const.tile([P, RUN, 2, DR // 2], F32)
-        sin_t = const.tile([P, RUN, 2, DR // 2], F32)
+        turns = const.tile([P, RUN, DR // 2], F32)
+        whole = const.tile([P, RUN, DR // 2], I32)
+        whole_f = const.tile([P, RUN, DR // 2], F32)
+        frac = const.tile([P, RUN, DR // 2], F32)
+        half = const.tile([P, RUN, DR // 2], F32)
+        cos_t = const.tile([P, RUN, DR // 2], F32)
+        sin_t = const.tile([P, RUN, DR // 2], F32)
         dummy = const.tile([P, 1], F32)
         xsc = const.tile([P, G1, 4], F32)
         wd_raw = const.tile([P, G1, DL], I32, align_bytes=64)
@@ -69,44 +73,42 @@ def tile_multilatentattention_pa_t_w8_kernel(tc, x_bytes, x_scale, wd_w, wd_s, w
         for i in range(UT):
             nc.sync.dma_start(out=xb[0][:, i, :], in_=b0[:, i, :])
         nc.sync.dma_start(out=xsc[:], in_=x_scale.rearrange("a b (g p t) -> p (a b g) t", p=P, t=4))
+        nc.vector.memset(sraw[:].bitcast(I32), 0)
+        load_x(1)
         for g in range(G1):
             nc.sync.dma_start(out=wd_raw[:, g, :], in_=wd_w[g].rearrange("p n t -> p (n t)").bitcast(I32))
-        nc.vector.memset(sraw[:].bitcast(I32), 0)
         for q in range(4):
             nc.sync.dma_start(out=sraw[32 * q:32 * q + 8, 0:DL].bitcast(I32), in_=wd_s.bitcast(I32)[:, 4 * q:4 * q + 4, :])
         for q in range(4):
             nc.sync.dma_start(out=sraw[32 * q:32 * q + 4, DL:].bitcast(I32), in_=wu_s.bitcast(I32)[0, 4 * q:4 * q + 4, :])
-        load_x(1)
+        load_x(2)
         wu_v = wu_w[0].rearrange("p n t -> p (n t)").bitcast(I32).rearrange("p (h f) -> p h f", h=H)
         for c0, c1, f0 in ((0, 256, 0), (256, 512, DH + DR), (512, 640, DH)):
             w = (c1 - c0) // 2
             nc.sync.dma_start(out=wu[:, c0:c1].rearrange("p (h d) -> p h d", h=H), in_=wu_v[:, :, f0:f0 + w])
-        for u in range(2, UNITS):
+        for u in range(3, UNITS):
             load_x(u)
 
-        make_identity(nc, ident[:])
         nc.gpsimd.iota(pos[:], pattern=[[1, RUN]], base=0, channel_multiplier=RUN)
+        make_identity(nc, ident[:])
         nc.vector.memset(dummy[:], 0.0)
         nc.scalar.activation(dummy[:], dummy[:], SIN)
-        nc.vector.tensor_scalar(out=turns[:, 0, :, 0], in0=pos[:], scalar1=1.0 / (2.0 * math.pi), scalar2=None, op0=MULT)
-        n = 1
-        while n < DR // 2:
-            nc.gpsimd.tensor_scalar(out=turns[:, 0, :, n:2 * n], in0=turns[:, 0, :, 0:n], scalar1=10000.0 ** (-n / 32.0), scalar2=0.0, op0=MULT, op1=ADD)
-            n *= 2
-        nc.gpsimd.tensor_scalar(out=turns[:, 1], in0=turns[:, 0], scalar1=1.0, scalar2=0.25, op0=MULT, op1=ADD)
+        for n in range(4):
+            nc.vector.tensor_scalar(out=turns[:, :, n], in0=pos[:], scalar1=10000.0 ** (-n / 32.0) / (2.0 * math.pi), scalar2=None, op0=MULT)
+        for n in (4, 8, 16):
+            nc.vector.tensor_scalar(out=turns[:, :, n:2 * n], in0=turns[:, :, 0:n], scalar1=10000.0 ** (-n / 32.0), scalar2=None, op0=MULT)
+        nc.vector.tensor_copy(out=whole[:], in_=turns[:])
+        nc.vector.tensor_copy(out=whole_f[:], in_=whole[:])
+        nc.gpsimd.tensor_tensor(out=frac[:], in0=turns[:], in1=whole_f[:], op=SUB)
 
-        def tables_v():
-            nc.vector.tensor_copy(out=whole[:], in_=turns[:])
-            nc.vector.tensor_tensor(out=frac[:], in0=turns[:], in1=whole[:], op=SUB)
+        def tables():
+            nc.scalar.activation(sin_t[:], frac[:], SIN, scale=2.0 * math.pi)
+            nc.scalar.activation(half[:], frac[:], SIN, scale=math.pi)
+            nc.gpsimd.tensor_tensor(out=half[:], in0=half[:], in1=half[:], op=MULT)
+            nc.gpsimd.tensor_scalar(out=cos_t[:], in0=half[:], scalar1=-2.0, scalar2=1.0, op0=MULT, op1=ADD)
 
-        def tables_s():
-            for half in range(2):
-                nc.scalar.activation(cos_t[:, :, half, :], frac[:, 1], SIN, scale=2.0 * math.pi)
-                nc.scalar.activation(sin_t[:, :, half, :], frac[:, 0], SIN, scale=(2.0 * half - 1.0) * 2.0 * math.pi)
-
-        def permute_wd():
-            for g in range(G1):
-                nc.vector.tensor_copy(out=wd[:, g, :].rearrange("p (t m) -> p t m", t=4), in_=wd_raw[:, g, :].rearrange("p (m t) -> p t m", t=4))
+        def permute_wd(eng, g):
+            eng.tensor_copy(out=wd[:, g, :].rearrange("p (t m) -> p t m", t=4), in_=wd_raw[:, g, :].rearrange("p (m t) -> p t m", t=4))
 
         def permute_scales():
             nc.vector.tensor_copy(out=wds[:].rearrange("p (t m) -> p t m", t=4), in_=sraw[:, 0:DL].rearrange("p (m t) -> p t m", t=4))
@@ -115,21 +117,27 @@ def tile_multilatentattention_pa_t_w8_kernel(tc, x_bytes, x_scale, wd_w, wd_s, w
             sv = sraw[:, DL:].rearrange("p (h f) -> p h f", h=H)
             for c0, c1, f0 in ((0, 256, 0), (256, 512, DH + DR), (512, 640, DH)):
                 w = (c1 - c0) // 2
-                nc.vector.tensor_copy(out=wus[:, c0:c1].rearrange("p (h d) -> p h d", h=H), in_=sv[:, :, f0:f0 + w])
+                nc.gpsimd.tensor_copy(out=wus[:, c0:c1].rearrange("p (h d) -> p h d", h=H), in_=sv[:, :, f0:f0 + w])
 
         def cast(u):
-            xw[u] = work.tile([P, UT, D], BF16, name="xw")
-            for i in range(UT):
-                src = xb[u][:, i, :].bitcast(FP8)
-                if u == 0 and i == 0:
-                    nc.vector.tensor_copy(out=xw[u][:, i, :], in_=src)
-                else:
-                    nc.scalar.copy(out=xw[u][:, i, :], in_=src)
+            xw[u] = wide.tile([P, UT, D], BF16, name="xw")
+            for g in range(G1 if u == 0 else 1):
+                for i in range(UT):
+                    k = slice(512 * g, 512 * g + 512) if u == 0 else slice(0, D)
+                    src, dst = xb[u][:, i, k].bitcast(FP8), xw[u][:, i, k]
+                    if u == 0 and i == 0:
+                        nc.vector.tensor_copy(out=dst, in_=src)
+                    elif i == 1 and u in GPSIMD_CASTS:
+                        for q in range(4):
+                            k = slice(256 * q, 256 * q + 256)
+                            nc.gpsimd.tensor_copy(out=xw[u][:, i, k], in_=xb[u][:, i, k].bitcast(FP8))
+                    else:
+                        nc.scalar.copy(out=dst, in_=src)
 
         def transpose(u):
             for g in range(G1):
                 xt[u, g] = ps_x.tile([P, 2, TOK], F32, name="xt")
-            order = [(g, i) for g in range(G1) for i in range(UT)] if u else [(g, i) for i in range(UT) for g in range(G1)]
+            order = [(g, i) for g in range(G1) for i in range(UT)]
             for g, i in order:
                     words = xw[u][:, i, :].bitcast(F32)
                     for w in range(2):
@@ -167,19 +175,26 @@ def tile_multilatentattention_pa_t_w8_kernel(tc, x_bytes, x_scale, wd_w, wd_s, w
                 copy = nc.vector.tensor_copy if u == UNITS - 1 and i == 1 else nc.scalar.copy
                 copy(out=lat[u][:, i], in_=lt[u, i][:].rearrange("p t n -> p n t"))
 
-        def quantize_latent(u):
-            lq[u] = work.tile([P, TOK], I32, name="lq", align_bytes=64)
-            lqs[u] = work.tile([P, TOK], U8, name="lqs", align_bytes=64)
-            nc.vector.quantize_mx(out=lq[u][:].bitcast(FP8X4), scales=lqs[u][:], in_=lat[u][:].rearrange("p i n t -> p (i n t)"))
+        def quantize_latent(u, tiles):
+            if tiles[0] == 0:
+                lq[u] = work.tile([P, TOK], I32, name="lq", align_bytes=64)
+                lqs[u] = work.tile([P, TOK], U8, name="lqs", align_bytes=64)
+            c = slice(tiles[0] * P, (tiles[-1] + 1) * P)
+            nc.vector.quantize_mx(out=lq[u][:, c].bitcast(FP8X4), scales=lqs[u][:, c],
+                                  in_=lat[u][:, tiles[0]:tiles[-1] + 1].rearrange("p i n t -> p (i n t)"))
 
         def project_up(u):
             rb[u] = ps_r.tile([P, UT, H * DR], F32, name="rb")
+            jobs = []
             for i in range(UT):
                 mb[u, i] = ps_m.tile([P, 512], F32, name="mb")
+                jobs += [(i, mb[u, i][:], slice(0, 512)), (i, rb[u][:, i, :], slice(512, 640))]
+            if u == UNITS - 1:
+                jobs = jobs[0::2] + jobs[1::2]
+            for i, out, cols in jobs:
                 c = slice(i * P, (i + 1) * P)
-                for out, cols in ((rb[u][:, i, :], slice(512, 640)), (mb[u, i][:], slice(0, 512))):
-                    nc.tensor.matmul_mx(out=out, lhsT=lq[u][:, c].bitcast(FP8X4), lhsT_scale=lqs[u][:, c],
-                                        rhs=wu[:, cols].bitcast(FP8X4), rhs_scale=wus[:, cols], start=True, stop=True)
+                nc.tensor.matmul_mx(out=out, lhsT=lq[u][:, c].bitcast(FP8X4), lhsT_scale=lqs[u][:, c],
+                                    rhs=wu[:, cols].bitcast(FP8X4), rhs_scale=wus[:, cols], start=True, stop=True)
 
         def evac_main(u):
             st[u] = stage.tile([P, UT, 4, SLOT], F32, name="st")
@@ -189,23 +204,20 @@ def tile_multilatentattention_pa_t_w8_kernel(tc, x_bytes, x_scale, wd_w, wd_s, w
                 copy(out=st[u][:, i, :, 0:DH], in_=mb[u, i][:].rearrange("p (s d) -> p s d", s=4))
                 nc.sync.dma_start(out=out_v[b].rearrange("(r i) h d -> r i h d", i=RUN)[:, UT * j + i], in_=st[u][:, i, 2:4, 0:DH])
 
-        def rope_mult(u, part):
+        def rope_mult(u, table, name, dst):
             j = u % NPOS
-            v = rb[u][:].rearrange("p i (h a d) -> p i h a d", h=H, a=2)
-            shape = [P, UT, H, 2, DR // 2]
-            if part == 0:
-                ra[u] = work.tile(shape, F32, name="ra")
-                tc_ = cos_t[:, UT * j:UT * (j + 1)].unsqueeze(2).to_broadcast(shape)
-                nc.vector.tensor_tensor(out=ra[u][:], in0=v, in1=tc_, op=MULT)
-            else:
-                rs[u] = work.tile(shape, F32, name="rs")
-                ts_ = sin_t[:, UT * j:UT * (j + 1)].unsqueeze(2).to_broadcast(shape)
-                nc.vector.tensor_tensor(out=rs[u][:], in0=v[:, :, :, ::-1, :], in1=ts_, op=MULT)
+            shape = [P, UT, 2 * H, DR // 2]
+            dst[u] = work.tile(shape, F32, name=name)
+            nc.vector.tensor_tensor(out=dst[u][:], in0=rb[u][:].rearrange("p i (x d) -> p i x d", x=2 * H),
+                                    in1=table[:, UT * j:UT * (j + 1)].unsqueeze(2).to_broadcast(shape), op=MULT)
 
         def rope_add(u):
             b, j = divmod(u, NPOS)
-            nc.gpsimd.tensor_tensor(out=st[u][:, :, 0:2, DH:SLOT], in0=ra[u][:].rearrange("p i h a d -> p i h (a d)"),
-                                    in1=rs[u][:].rearrange("p i h a d -> p i h (a d)"), op=ADD)
+            a = ra[u][:].rearrange("p i (h a) d -> p i h a d", a=2)
+            c = rs[u][:].rearrange("p i (h a) d -> p i h a d", a=2)
+            for k, op in ((0, SUB), (1, ADD)):
+                f = DH + k * (DR // 2)
+                nc.gpsimd.tensor_tensor(out=st[u][:, :, 0:2, f:f + DR // 2], in0=a[:, :, :, k, :], in1=c[:, :, :, 1 - k, :], op=op)
             nc.sync.dma_start(out=out_k[b].rearrange("(r i) h d -> r i (h d)", i=RUN)[:, UT * j:UT * (j + 1), :],
                               in_=st[u][:, :, 0:2, :].rearrange("p i s d -> p i (s d)"))
 
@@ -214,30 +226,35 @@ def tile_multilatentattention_pa_t_w8_kernel(tc, x_bytes, x_scale, wd_w, wd_s, w
 
         cast(0)
         cast(1)
-        permute_wd()
-        tables_v()
         transpose(0)
-        tables_s()
+        permute_wd(nc.gpsimd, 0)
+        cast(2)
+        tables()
+        permute_wus()
         for s in range(UNITS + 2):
-            if ok(s + 2):
-                cast(s + 2)
+            if ok(s + 3):
+                cast(s + 3)
             if ok(s):
                 scale(s, 0)
                 scale(s, 1)
                 if s == 0:
+                    permute_wd(nc.vector, 1)
                     permute_scales()
                 quantize_x(s, 0)
-            if ok(s - 2):
-                rope_mult(s - 2, 0)
+            if ok(s - 2) and s - 2 < UNITS - 2:
+                rope_mult(s - 2, cos_t, "ra", ra)
             if ok(s):
                 quantize_x(s, 1)
-            if ok(s - 2):
-                rope_mult(s - 2, 1)
+            if ok(s - 2) and s - 2 < UNITS - 2:
+                rope_mult(s - 2, sin_t, "rs", rs)
                 rope_add(s - 2)
-            if s == 0:
-                permute_wus()
             if ok(s - 1):
-                quantize_latent(s - 1)
+                for tiles in ((0, 1),) if s < UNITS else ((0,), (1,)):
+                    quantize_latent(s - 1, tiles)
+            if ok(s - 2) and s - 2 >= UNITS - 2:
+                rope_mult(s - 2, cos_t, "ra", ra)
+                rope_mult(s - 2, sin_t, "rs", rs)
+                rope_add(s - 2)
             if ok(s + 1):
                 transpose(s + 1)
             if ok(s):

@@ -24,7 +24,7 @@ TOK = UT * P
 UNITS = B * RUN // UT
 NPOS = RUN // UT
 SLOT = DH + DR
-GPSIMD_CASTS = (3, 4, 6, 8, 9, 11, 13, 15)
+GPSIMD_CASTS = ()
 
 FLOPS = 2 * B * S * (D * DL + DL * H * (2 * DH + DR))
 
@@ -61,7 +61,7 @@ def tile_multilatentattention_pa_t_w8_kernel(tc, x_bytes, x_scale, wd_w, wd_s, w
         wu = const.tile([P, 640], I32, align_bytes=64)
         wus = const.tile([P, 640], U8, align_bytes=64)
 
-        xb, xw, xt, xs, xq, xqs, lt, lat, lq, lqs, mb, rb, st, ra, rs = [{} for _ in range(15)]
+        xb, xw, xt, xs, xq, xqs, lt, lat, lq, lqs, mb, rb, re, st, ra, rs = [{} for _ in range(16)]
 
         def load_x(u):
             xb[u] = xin.tile([P, UT, D], U8, name="xb")
@@ -152,11 +152,11 @@ def tile_multilatentattention_pa_t_w8_kernel(tc, x_bytes, x_scale, wd_w, wd_s, w
                 in1=xsc[:, g, :].rearrange("p (w e) -> p w e", e=2).unsqueeze(1).to_broadcast([P, TOK, 2, 2]),
                 op=MULT)
 
-        def quantize_x(u, g):
-            if g == 0:
-                xq[u] = work.tile([P, G1, TOK], I32, name="xq", align_bytes=64)
-                xqs[u] = work.tile([P, G1, TOK], U8, name="xqs", align_bytes=64)
-            nc.vector.quantize_mx(out=xq[u][:, g, :].bitcast(FP8X4), scales=xqs[u][:, g, :], in_=xs[u][:, g].rearrange("p n t -> p (n t)"))
+        def quantize_x(u):
+            xq[u] = work.tile([P, G1, TOK], I32, name="xq", align_bytes=64)
+            xqs[u] = work.tile([P, G1, TOK], U8, name="xqs", align_bytes=64)
+            nc.vector.quantize_mx(out=xq[u][:].rearrange("p g n -> p (g n)").bitcast(FP8X4), scales=xqs[u][:].rearrange("p g n -> p (g n)"),
+                                  in_=xs[u][:].rearrange("p g n t -> p (g n t)"))
 
         def project_down(u):
             for i in range(UT):
@@ -204,22 +204,33 @@ def tile_multilatentattention_pa_t_w8_kernel(tc, x_bytes, x_scale, wd_w, wd_s, w
                 copy(out=st[u][:, i, :, 0:DH], in_=mb[u, i][:].rearrange("p (s d) -> p s d", s=4))
                 nc.sync.dma_start(out=out_v[b].rearrange("(r i) h d -> r i h d", i=RUN)[:, UT * j + i], in_=st[u][:, i, 2:4, 0:DH])
 
-        def rope_mult(u, table, name, dst):
+        def evac_rope(u):
+            re[u] = work.tile([P, UT, 2 * H, DR // 2], F32, name="re")
+            nc.scalar.copy(out=re[u][:].rearrange("p i x d -> p (i x d)"), in_=rb[u][:].rearrange("p i x -> p (i x)"))
+
+        def rope_mult(u, eng, src):
             j = u % NPOS
             shape = [P, UT, 2 * H, DR // 2]
-            dst[u] = work.tile(shape, F32, name=name)
-            nc.vector.tensor_tensor(out=dst[u][:], in0=rb[u][:].rearrange("p i (x d) -> p i x d", x=2 * H),
-                                    in1=table[:, UT * j:UT * (j + 1)].unsqueeze(2).to_broadcast(shape), op=MULT)
+            for table, name, dst in ((cos_t, "ra", ra), (sin_t, "rs", rs)):
+                dst[u] = work.tile(shape, F32, name=name)
+                eng.tensor_tensor(out=dst[u][:], in0=src, in1=table[:, UT * j:UT * (j + 1)].unsqueeze(2).to_broadcast(shape), op=MULT)
 
-        def rope_add(u):
+        def rope_add(u, eng):
             b, j = divmod(u, NPOS)
             a = ra[u][:].rearrange("p i (h a) d -> p i h a d", a=2)
             c = rs[u][:].rearrange("p i (h a) d -> p i h a d", a=2)
             for k, op in ((0, SUB), (1, ADD)):
                 f = DH + k * (DR // 2)
-                nc.gpsimd.tensor_tensor(out=st[u][:, :, 0:2, f:f + DR // 2], in0=a[:, :, :, k, :], in1=c[:, :, :, 1 - k, :], op=op)
+                eng.tensor_tensor(out=st[u][:, :, 0:2, f:f + DR // 2], in0=a[:, :, :, k, :], in1=c[:, :, :, 1 - k, :], op=op)
             nc.sync.dma_start(out=out_k[b].rearrange("(r i) h d -> r i (h d)", i=RUN)[:, UT * j:UT * (j + 1), :],
                               in_=st[u][:, :, 0:2, :].rearrange("p i s d -> p i (s d)"))
+
+        def rope(u):
+            if u < UNITS - 2:
+                rope_mult(u, nc.gpsimd, re[u][:])
+            else:
+                rope_mult(u, nc.vector, rb[u][:].rearrange("p i (x d) -> p i x d", x=2 * H))
+            rope_add(u, nc.vector if u == UNITS - 1 else nc.gpsimd)
 
         def ok(u):
             return 0 <= u < UNITS
@@ -240,21 +251,12 @@ def tile_multilatentattention_pa_t_w8_kernel(tc, x_bytes, x_scale, wd_w, wd_s, w
                 if s == 0:
                     permute_wd(nc.vector, 1)
                     permute_scales()
-                quantize_x(s, 0)
-            if ok(s - 2) and s - 2 < UNITS - 2:
-                rope_mult(s - 2, cos_t, "ra", ra)
-            if ok(s):
-                quantize_x(s, 1)
-            if ok(s - 2) and s - 2 < UNITS - 2:
-                rope_mult(s - 2, sin_t, "rs", rs)
-                rope_add(s - 2)
+                quantize_x(s)
             if ok(s - 1):
                 for tiles in ((0, 1),) if s < UNITS else ((0,), (1,)):
                     quantize_latent(s - 1, tiles)
-            if ok(s - 2) and s - 2 >= UNITS - 2:
-                rope_mult(s - 2, cos_t, "ra", ra)
-                rope_mult(s - 2, sin_t, "rs", rs)
-                rope_add(s - 2)
+            if ok(s - 2):
+                rope(s - 2)
             if ok(s + 1):
                 transpose(s + 1)
             if ok(s):
@@ -263,3 +265,5 @@ def tile_multilatentattention_pa_t_w8_kernel(tc, x_bytes, x_scale, wd_w, wd_s, w
             if ok(s - 1):
                 project_up(s - 1)
                 evac_main(s - 1)
+                if s - 1 < UNITS - 2:
+                    evac_rope(s - 1)

import math
from contextlib import ExitStack

import concourse.mybir as mybir
from concourse.masks import make_identity

F32 = mybir.dt.float32
BF16 = mybir.dt.bfloat16
I32 = mybir.dt.int32
U8 = mybir.dt.uint8
FP8 = mybir.dt.float8_e4m3fn
FP8X4 = mybir.dt.float8_e4m3fn_x4
ADD = mybir.AluOpType.add
SUB = mybir.AluOpType.subtract
MULT = mybir.AluOpType.mult
SIN = mybir.ActivationFunctionType.Sin

P = 128
B, S, D, H, DH, DL, DR = 2, 2048, 1024, 2, 128, 512, 64
G1 = D // 512
RUN = S // P
UT = 2
TOK = UT * P
UNITS = B * RUN // UT
NPOS = RUN // UT
SLOT = DH + DR
GPSIMD_CASTS = ()

FLOPS = 2 * B * S * (D * DL + DL * H * (2 * DH + DR))


def tile_multilatentattention_pa_t_w8_kernel(tc, x_bytes, x_scale, wd_w, wd_s, wu_w, wu_s, out_k, out_v):
    nc = tc.nc
    with ExitStack() as ctx:
        const = ctx.enter_context(tc.tile_pool(name="const", bufs=1))
        xin = ctx.enter_context(tc.tile_pool(name="xin", bufs=UNITS))
        work = ctx.enter_context(tc.tile_pool(name="work", bufs=4))
        wide = ctx.enter_context(tc.tile_pool(name="wide", bufs=5))
        stage = ctx.enter_context(tc.tile_pool(name="stage", bufs=4))
        ps_x = ctx.enter_context(tc.psum_pool(name="ps_x", bufs=3))
        ps_l = ctx.enter_context(tc.psum_pool(name="ps_l", bufs=2))
        ps_m = ctx.enter_context(tc.psum_pool(name="ps_m", bufs=2))
        ps_r = ctx.enter_context(tc.psum_pool(name="ps_r", bufs=1))
        ctx.enter_context(tc.manual_schedule())

        ident = const.tile([P, P], F32)
        pos = const.tile([P, RUN], I32)
        turns = const.tile([P, RUN, DR // 2], F32)
        whole = const.tile([P, RUN, DR // 2], I32)
        whole_f = const.tile([P, RUN, DR // 2], F32)
        frac = const.tile([P, RUN, DR // 2], F32)
        half = const.tile([P, RUN, DR // 2], F32)
        cos_t = const.tile([P, RUN, DR // 2], F32)
        sin_t = const.tile([P, RUN, DR // 2], F32)
        dummy = const.tile([P, 1], F32)
        xsc = const.tile([P, G1, 4], F32)
        wd_raw = const.tile([P, G1, DL], I32, align_bytes=64)
        wd = const.tile([P, G1, DL], I32, align_bytes=64)
        sraw = const.tile([P, DL + 640], U8, align_bytes=64)
        wds = const.tile([P, DL], U8, align_bytes=64)
        wu = const.tile([P, 640], I32, align_bytes=64)
        wus = const.tile([P, 640], U8, align_bytes=64)

        xb, xw, xt, xs, xq, xqs, lt, lat, lq, lqs, mb, rb, re, st, ra, rs = [{} for _ in range(16)]

        def load_x(u):
            xb[u] = xin.tile([P, UT, D], U8, name="xb")
            b, j = divmod(u, NPOS)
            nc.sync.dma_start(out=xb[u][:], in_=x_bytes[b].rearrange("(r i) k -> r i k", i=RUN)[:, UT * j:UT * (j + 1), :])

        b0 = x_bytes[0].rearrange("(r i) k -> r i k", i=RUN)
        xb[0] = xin.tile([P, UT, D], U8, name="xb")
        for i in range(UT):
            nc.sync.dma_start(out=xb[0][:, i, :], in_=b0[:, i, :])
        nc.sync.dma_start(out=xsc[:], in_=x_scale.rearrange("a b (g p t) -> p (a b g) t", p=P, t=4))
        nc.vector.memset(sraw[:].bitcast(I32), 0)
        load_x(1)
        for g in range(G1):
            nc.sync.dma_start(out=wd_raw[:, g, :], in_=wd_w[g].rearrange("p n t -> p (n t)").bitcast(I32))
        for q in range(4):
            nc.sync.dma_start(out=sraw[32 * q:32 * q + 8, 0:DL].bitcast(I32), in_=wd_s.bitcast(I32)[:, 4 * q:4 * q + 4, :])
        for q in range(4):
            nc.sync.dma_start(out=sraw[32 * q:32 * q + 4, DL:].bitcast(I32), in_=wu_s.bitcast(I32)[0, 4 * q:4 * q + 4, :])
        load_x(2)
        wu_v = wu_w[0].rearrange("p n t -> p (n t)").bitcast(I32).rearrange("p (h f) -> p h f", h=H)
        for c0, c1, f0 in ((0, 256, 0), (256, 512, DH + DR), (512, 640, DH)):
            w = (c1 - c0) // 2
            nc.sync.dma_start(out=wu[:, c0:c1].rearrange("p (h d) -> p h d", h=H), in_=wu_v[:, :, f0:f0 + w])
        for u in range(3, UNITS):
            load_x(u)

        nc.gpsimd.iota(pos[:], pattern=[[1, RUN]], base=0, channel_multiplier=RUN)
        make_identity(nc, ident[:])
        nc.vector.memset(dummy[:], 0.0)
        nc.scalar.activation(dummy[:], dummy[:], SIN)
        for n in range(4):
            nc.vector.tensor_scalar(out=turns[:, :, n], in0=pos[:], scalar1=10000.0 ** (-n / 32.0) / (2.0 * math.pi), scalar2=None, op0=MULT)
        for n in (4, 8, 16):
            nc.vector.tensor_scalar(out=turns[:, :, n:2 * n], in0=turns[:, :, 0:n], scalar1=10000.0 ** (-n / 32.0), scalar2=None, op0=MULT)
        nc.vector.tensor_copy(out=whole[:], in_=turns[:])
        nc.vector.tensor_copy(out=whole_f[:], in_=whole[:])
        nc.gpsimd.tensor_tensor(out=frac[:], in0=turns[:], in1=whole_f[:], op=SUB)

        def tables():
            nc.scalar.activation(sin_t[:], frac[:], SIN, scale=2.0 * math.pi)
            nc.scalar.activation(half[:], frac[:], SIN, scale=math.pi)
            nc.gpsimd.tensor_tensor(out=half[:], in0=half[:], in1=half[:], op=MULT)
            nc.gpsimd.tensor_scalar(out=cos_t[:], in0=half[:], scalar1=-2.0, scalar2=1.0, op0=MULT, op1=ADD)

        def permute_wd(eng, g):
            eng.tensor_copy(out=wd[:, g, :].rearrange("p (t m) -> p t m", t=4), in_=wd_raw[:, g, :].rearrange("p (m t) -> p t m", t=4))

        def permute_scales():
            nc.vector.tensor_copy(out=wds[:].rearrange("p (t m) -> p t m", t=4), in_=sraw[:, 0:DL].rearrange("p (m t) -> p t m", t=4))

        def permute_wus():
            sv = sraw[:, DL:].rearrange("p (h f) -> p h f", h=H)
            for c0, c1, f0 in ((0, 256, 0), (256, 512, DH + DR), (512, 640, DH)):
                w = (c1 - c0) // 2
                nc.gpsimd.tensor_copy(out=wus[:, c0:c1].rearrange("p (h d) -> p h d", h=H), in_=sv[:, :, f0:f0 + w])

        def cast(u):
            xw[u] = wide.tile([P, UT, D], BF16, name="xw")
            for g in range(G1 if u == 0 else 1):
                for i in range(UT):
                    k = slice(512 * g, 512 * g + 512) if u == 0 else slice(0, D)
                    src, dst = xb[u][:, i, k].bitcast(FP8), xw[u][:, i, k]
                    if u == 0 and i == 0:
                        nc.vector.tensor_copy(out=dst, in_=src)
                    elif i == 1 and u in GPSIMD_CASTS:
                        for q in range(4):
                            k = slice(256 * q, 256 * q + 256)
                            nc.gpsimd.tensor_copy(out=xw[u][:, i, k], in_=xb[u][:, i, k].bitcast(FP8))
                    else:
                        nc.scalar.copy(out=dst, in_=src)

        def transpose(u):
            for g in range(G1):
                xt[u, g] = ps_x.tile([P, 2, TOK], F32, name="xt")
            order = [(g, i) for g in range(G1) for i in range(UT)]
            for g, i in order:
                    words = xw[u][:, i, :].bitcast(F32)
                    for w in range(2):
                        nc.tensor.transpose(xt[u, g][:, w, i * P:(i + 1) * P], words[:, 256 * g + w:256 * (g + 1):2], ident[:])

        def scale(u, g):
            if g == 0:
                xs[u] = work.tile([P, G1, TOK, 4], BF16, name="xs", align_bytes=64)
            nc.vector.tensor_tensor(
                out=xs[u][:, g].rearrange("p n (w e) -> p n w e", e=2),
                in0=xt[u, g][:].bitcast(BF16).rearrange("p w (n e) -> p n w e", e=2),
                in1=xsc[:, g, :].rearrange("p (w e) -> p w e", e=2).unsqueeze(1).to_broadcast([P, TOK, 2, 2]),
                op=MULT)

        def quantize_x(u):
            xq[u] = work.tile([P, G1, TOK], I32, name="xq", align_bytes=64)
            xqs[u] = work.tile([P, G1, TOK], U8, name="xqs", align_bytes=64)
            nc.vector.quantize_mx(out=xq[u][:].rearrange("p g n -> p (g n)").bitcast(FP8X4), scales=xqs[u][:].rearrange("p g n -> p (g n)"),
                                  in_=xs[u][:].rearrange("p g n t -> p (g n t)"))

        def project_down(u):
            for i in range(UT):
                lt[u, i] = ps_l.tile([P, 4, P], F32, name="lt")
                c = slice(i * P, (i + 1) * P)
                for t in range(4):
                    m = slice(t * P, (t + 1) * P)
                    for g in range(G1):
                        nc.tensor.matmul_mx(out=lt[u, i][:, t, :], lhsT=wd[:, g, m].bitcast(FP8X4), lhsT_scale=wds[4 * g:P, m],
                                            rhs=xq[u][:, g, c].bitcast(FP8X4), rhs_scale=xqs[u][:, g, c],
                                            start=(g == 0), stop=(g == G1 - 1))

        def evac_latent(u):
            lat[u] = work.tile([P, UT, P, 4], BF16, name="lat", align_bytes=64)
            for i in range(UT):
                copy = nc.vector.tensor_copy if u == UNITS - 1 and i == 1 else nc.scalar.copy
                copy(out=lat[u][:, i], in_=lt[u, i][:].rearrange("p t n -> p n t"))

        def quantize_latent(u, tiles):
            if tiles[0] == 0:
                lq[u] = work.tile([P, TOK], I32, name="lq", align_bytes=64)
                lqs[u] = work.tile([P, TOK], U8, name="lqs", align_bytes=64)
            c = slice(tiles[0] * P, (tiles[-1] + 1) * P)
            nc.vector.quantize_mx(out=lq[u][:, c].bitcast(FP8X4), scales=lqs[u][:, c],
                                  in_=lat[u][:, tiles[0]:tiles[-1] + 1].rearrange("p i n t -> p (i n t)"))

        def project_up(u):
            rb[u] = ps_r.tile([P, UT, H * DR], F32, name="rb")
            jobs = []
            for i in range(UT):
                mb[u, i] = ps_m.tile([P, 512], F32, name="mb")
                jobs += [(i, mb[u, i][:], slice(0, 512)), (i, rb[u][:, i, :], slice(512, 640))]
            if u == UNITS - 1:
                jobs = jobs[0::2] + jobs[1::2]
            for i, out, cols in jobs:
                c = slice(i * P, (i + 1) * P)
                nc.tensor.matmul_mx(out=out, lhsT=lq[u][:, c].bitcast(FP8X4), lhsT_scale=lqs[u][:, c],
                                    rhs=wu[:, cols].bitcast(FP8X4), rhs_scale=wus[:, cols], start=True, stop=True)

        def evac_main(u):
            st[u] = stage.tile([P, UT, 4, SLOT], F32, name="st")
            b, j = divmod(u, NPOS)
            for i in range(UT):
                copy = nc.vector.tensor_copy if u == UNITS - 1 and i == 1 else nc.scalar.copy
                copy(out=st[u][:, i, :, 0:DH], in_=mb[u, i][:].rearrange("p (s d) -> p s d", s=4))
                nc.sync.dma_start(out=out_v[b].rearrange("(r i) h d -> r i h d", i=RUN)[:, UT * j + i], in_=st[u][:, i, 2:4, 0:DH])

        def evac_rope(u):
            re[u] = work.tile([P, UT, 2 * H, DR // 2], F32, name="re")
            nc.scalar.copy(out=re[u][:].rearrange("p i x d -> p (i x d)"), in_=rb[u][:].rearrange("p i x -> p (i x)"))

        def rope_mult(u, eng, src):
            j = u % NPOS
            shape = [P, UT, 2 * H, DR // 2]
            for table, name, dst in ((cos_t, "ra", ra), (sin_t, "rs", rs)):
                dst[u] = work.tile(shape, F32, name=name)
                eng.tensor_tensor(out=dst[u][:], in0=src, in1=table[:, UT * j:UT * (j + 1)].unsqueeze(2).to_broadcast(shape), op=MULT)

        def rope_add(u, eng):
            b, j = divmod(u, NPOS)
            a = ra[u][:].rearrange("p i (h a) d -> p i h a d", a=2)
            c = rs[u][:].rearrange("p i (h a) d -> p i h a d", a=2)
            for k, op in ((0, SUB), (1, ADD)):
                f = DH + k * (DR // 2)
                eng.tensor_tensor(out=st[u][:, :, 0:2, f:f + DR // 2], in0=a[:, :, :, k, :], in1=c[:, :, :, 1 - k, :], op=op)
            nc.sync.dma_start(out=out_k[b].rearrange("(r i) h d -> r i (h d)", i=RUN)[:, UT * j:UT * (j + 1), :],
                              in_=st[u][:, :, 0:2, :].rearrange("p i s d -> p i (s d)"))

        def rope(u):
            if u < UNITS - 2:
                rope_mult(u, nc.gpsimd, re[u][:])
            else:
                rope_mult(u, nc.vector, rb[u][:].rearrange("p i (x d) -> p i x d", x=2 * H))
            rope_add(u, nc.vector if u == UNITS - 1 else nc.gpsimd)

        def ok(u):
            return 0 <= u < UNITS

        cast(0)
        cast(1)
        transpose(0)
        permute_wd(nc.gpsimd, 0)
        cast(2)
        tables()
        permute_wus()
        for s in range(UNITS + 2):
            if ok(s + 3):
                cast(s + 3)
            if ok(s):
                scale(s, 0)
                scale(s, 1)
                if s == 0:
                    permute_wd(nc.vector, 1)
                    permute_scales()
                quantize_x(s)
            if ok(s - 1):
                for tiles in ((0, 1),) if s < UNITS else ((0,), (1,)):
                    quantize_latent(s - 1, tiles)
            if ok(s - 2):
                rope(s - 2)
            if ok(s + 1):
                transpose(s + 1)
            if ok(s):
                project_down(s)
                evac_latent(s)
            if ok(s - 1):
                project_up(s - 1)
                evac_main(s - 1)
                if s - 1 < UNITS - 2:
                    evac_rope(s - 1)
